import numpy as np
import ml_dtypes


def mxq(x, axis, fmt="e4m3"):
    dtype, down = {"e4m3": (ml_dtypes.float8_e4m3fn, 7), "e5m2": (ml_dtypes.float8_e5m2, 14)}[fmt]
    v = np.moveaxis(np.asarray(x, np.float32).astype(ml_dtypes.bfloat16).astype(np.float64), axis, -1)
    blocks = v.reshape(v.shape[:-1] + (-1, 32))
    amax = np.abs(blocks).max(-1, keepdims=True)
    byte = np.maximum(np.where(amax > 0, np.frexp(amax)[1] - 1 + 127, 0) - down, 1)
    scale = np.exp2(byte - 127.0)
    codes = (blocks / scale).astype(np.float32).astype(dtype).astype(np.float64)
    return np.moveaxis((codes * scale).reshape(v.shape), -1, axis)


WIDE = False


def mx_kscale(k):
    if not WIDE:
        return np.ones(k)
    levels = np.array([10, -10, 5, -5, 0])
    a = np.random.permutation(np.resize(levels, k // 512 * 4)).reshape(k // 512, 4)
    idx = np.arange(k)
    return np.exp2(a[idx // 512, idx % 128 // 32])


BF16 = ml_dtypes.bfloat16


def bf(x):
    return np.asarray(x, np.float32).astype(BF16)


def f64(x):
    return np.asarray(x).astype(np.float64)


B, S, IQ, OQ, Q = 4, 256, 512, 512, 4


def setup_inputs():
    s = mx_kscale(IQ)
    sw = 0.5 / np.sqrt(IQ)
    return {"x": bf((np.random.standard_normal((B, S, IQ, Q)) * s[:, None]).reshape(B, S, IQ * Q)),
            "wr": bf(np.random.standard_normal((OQ, IQ)) * sw / s),
            "wi": bf(np.random.standard_normal((OQ, IQ)) * sw / s),
            "wj": bf(np.random.standard_normal((OQ, IQ)) * sw / s),
            "wk": bf(np.random.standard_normal((OQ, IQ)) * sw / s),
            "bias": bf(np.random.standard_normal(OQ * Q) * 0.3)}


def reference(x, wr, wi, wj, wk, bias):
    xq = f64(x).reshape(B * S, IQ, Q)
    xr = mxq(xq[:, :, 0], 1, "e4m3")
    xi = mxq(xq[:, :, 1], 1, "e4m3")
    xj = mxq(xq[:, :, 2], 1, "e4m3")
    xk = mxq(xq[:, :, 3], 1, "e4m3")
    qr = mxq(f64(wr), 1, "e4m3")
    qi = mxq(f64(wi), 1, "e4m3")
    qj = mxq(f64(wj), 1, "e4m3")
    qk = mxq(f64(wk), 1, "e4m3")
    Ar = xr @ qr.T
    Br = xi @ qr.T
    Cr = xj @ qr.T
    Dr = xk @ qr.T
    Ai = xr @ qi.T
    Bi = xi @ qi.T
    Aj = xr @ qj.T
    Cj = xj @ qj.T
    Ak = xr @ qk.T
    Dk = xk @ qk.T
    or_ = Ar - Bi - Cj - Dk
    oi_ = Br + Ai + Dk - Cj
    oj_ = Cr - Dk + Aj + Bi
    ok_ = Dr + Cj - Bi + Ak
    out = np.stack([or_, oi_, oj_, ok_], axis=-1).reshape(B, S, Q * OQ)
    return out + f64(bias)[None, None, :]

@@ -1,0 +1,155 @@
+import concourse.mybir as mybir
+from concourse.masks import make_identity
+
+F32 = mybir.dt.float32
+BF16 = mybir.dt.bfloat16
+U32 = mybir.dt.uint32
+U8 = mybir.dt.uint8
+FP8X4 = mybir.dt.float8_e4m3fn_x4
+
+P = 128
+Q = 4
+ROWS = 1024
+IQ = 512
+OQ = 512
+ROW_TILES = ROWS // P
+O_BLOCKS = OQ // P
+WORDS = IQ // 2
+GROUPED = Q * P * 4
+
+FLOPS = 2 * ROWS * IQ * OQ * 10
+
+WR = 0
+WI = 1
+WJ = 2
+WK = 3
+NEG_WI = 4
+NEG_WJ = 5
+NEG_WK = 6
+SLOTS = 7
+
+WEIGHT_FOR = (
+    (WR, NEG_WI, NEG_WJ, NEG_WK),
+    (WI, WR, NEG_WJ, WK),
+    (WJ, WI, WR, NEG_WK),
+    (WK, NEG_WI, WJ, WR),
+)
+
+
+def tile_quaternionlinear_pa_kernel(tc, x, wr, wi, wj, wk, bias, out):
+    nc = tc.nc
+    x_rows = x.flatten_outer_dims()
+    out_rows = out.flatten_outer_dims()
+    weights = (wr, wi, wj, wk)
+
+    with tc.tile_pool(name="keep", bufs=1) as keep, tc.tile_pool(name="stage", bufs=3) as stage, tc.tile_pool(
+        name="results", bufs=4
+    ) as results, tc.psum_pool(name="flipped", bufs=4) as flipped, tc.psum_pool(name="sums", bufs=4) as sums:
+        w_raw = []
+        x_raw = []
+
+        def load_weights(ob):
+            block = keep.tile([P, Q, IQ], BF16, name="w_raw%d" % ob)
+            for m in range(Q):
+                nc.sync.dma_start(out=block[:, m, :], in_=weights[m][ob * P : (ob + 1) * P, :])
+            w_raw.append(block)
+
+        def load_x(t):
+            rows = keep.tile([P, IQ * Q], BF16, name="x_raw%d" % t)
+            nc.sync.dma_start(out=rows[:], in_=x_rows[t * P : (t + 1) * P, :])
+            x_raw.append(rows)
+
+        load_weights(0)
+        load_x(0)
+        for ob in range(1, O_BLOCKS):
+            load_weights(ob)
+        load_x(1)
+        bias_all = keep.tile([P, OQ * Q], BF16)
+        nc.sync.dma_start(out=bias_all[:], in_=bias.partition_broadcast(P))
+        for t in range(2, ROW_TILES):
+            load_x(t)
+
+        identity = keep.tile([P, P], F32)
+        make_identity(nc, identity[:])
+
+        w_codes = keep.tile([P, O_BLOCKS, SLOTS * P], U32, align_bytes=64)
+        w_scales = keep.tile([P, O_BLOCKS, SLOTS * P], U8, align_bytes=64)
+
+        def transpose_and_group(four):
+            words = four.bitcast(F32)
+            grouped = stage.tile([P, GROUPED], BF16, align_bytes=64)
+            grouped_words = grouped[:].bitcast(F32).rearrange("p (m r u) -> p m r u", m=Q, u=2)
+            for pair in range(2):
+                bank = flipped.tile([P, 2, 2, P], F32)
+                for m in range(2):
+                    for u in range(2):
+                        nc.tensor.transpose(bank[:, m, u, :], words[:, 2 * pair + m, u * P : (u + 1) * P], identity[:])
+                nc.scalar.copy(
+                    out=grouped_words[:, 2 * pair : 2 * pair + 2, :, :], in_=bank[:].rearrange("p m u r -> p m r u")
+                )
+            return grouped
+
+        def prepare_weights(ob):
+            grouped = transpose_and_group(w_raw[ob][:])
+            nc.vector.quantize_mx(
+                out=w_codes[:, ob, 0 : Q * P].bitcast(FP8X4), scales=w_scales[:, ob, 0 : Q * P], in_=grouped[:]
+            )
+            negated = stage.tile([P, 3 * P * 4], BF16, align_bytes=64)
+            nc.vector.tensor_scalar(
+                out=negated[:], in0=grouped[:, P * 4 :], scalar1=-1.0, scalar2=None, op0=mybir.AluOpType.mult
+            )
+            nc.vector.quantize_mx(
+                out=w_codes[:, ob, NEG_WI * P : NEG_WK * P].bitcast(FP8X4),
+                scales=w_scales[:, ob, NEG_WI * P : NEG_WK * P],
+                in_=negated[:, 0 : 2 * P * 4],
+            )
+            nc.vector.quantize_mx(
+                out=w_codes[:, ob, NEG_WK * P : SLOTS * P].bitcast(FP8X4),
+                scales=w_scales[:, ob, NEG_WK * P : SLOTS * P],
+                in_=negated[:, 2 * P * 4 :],
+            )
+
+        def prepare_x(t):
+            planes = stage.tile([P, Q, IQ], BF16)
+            interleaved = x_raw[t][:].rearrange("p (i c) -> p c i", c=Q)
+            nc.vector.tensor_copy(out=planes[:, 0:2, :], in_=interleaved[:, 0:2, :])
+            nc.scalar.copy(out=planes[:, 2:4, :], in_=interleaved[:, 2:4, :])
+            grouped = transpose_and_group(planes[:])
+            x_codes = stage.tile([P, Q * P], U32, align_bytes=64)
+            x_scales = stage.tile([P, Q * P], U8, align_bytes=64)
+            nc.vector.quantize_mx(out=x_codes[:].bitcast(FP8X4), scales=x_scales[:], in_=grouped[:])
+            return x_codes, x_scales
+
+        def multiply(t, x_codes, x_scales):
+            for ob in range(O_BLOCKS):
+                acc = sums.tile([P, Q, P], F32)
+                for c_out in range(Q):
+                    for c_in in range(Q):
+                        slot = WEIGHT_FOR[c_out][c_in]
+                        nc.tensor.matmul_mx(
+                            out=acc[:, c_out, :],
+                            lhsT=x_codes[:, c_in * P : (c_in + 1) * P].bitcast(FP8X4),
+                            lhsT_scale=x_scales[:, c_in * P : (c_in + 1) * P],
+                            rhs=w_codes[:, ob, slot * P : (slot + 1) * P].bitcast(FP8X4),
+                            rhs_scale=w_scales[:, ob, slot * P : (slot + 1) * P],
+                            start=(c_in == 0),
+                            stop=(c_in == Q - 1),
+                        )
+                cols = slice(ob * P * Q, (ob + 1) * P * Q)
+                result = results.tile([P, P * Q], F32)
+                nc.vector.tensor_tensor(
+                    out=result[:].rearrange("p (o c) -> p o c", c=Q),
+                    in0=acc[:].rearrange("p c o -> p o c"),
+                    in1=bias_all[:, cols].rearrange("p (o c) -> p o c", c=Q),
+                    op=mybir.AluOpType.add,
+                )
+                nc.sync.dma_start(out=out_rows[t * P : (t + 1) * P, cols], in_=result[:])
+
+        prepare_weights(0)
+        ready = prepare_x(0)
+        for ob in range(1, O_BLOCKS):
+            prepare_weights(ob)
+        for t in range(ROW_TILES):
+            following = prepare_x(t + 1) if t + 1 < ROW_TILES else None
+            multiply(t, ready[0], ready[1])
+            ready = following

@@ -13,9 +13,13 @@ ROWS = 1024
 IQ = 512
 OQ = 512
 ROW_TILES = ROWS // P
+PAIRS = ROW_TILES // 2
 O_BLOCKS = OQ // P
-WORDS = IQ // 2
-GROUPED = Q * P * 4
+MATRIX = P * 4
+BANK_BF16 = 1024
+MATMUL_COLS = 512
+DEINTERLEAVE_AT = 0
+TRANSPOSE_AT = 2
 
 FLOPS = 2 * ROWS * IQ * OQ * 10
 
@@ -26,7 +30,7 @@ WK = 3
 NEG_WI = 4
 NEG_WJ = 5
 NEG_WK = 6
-SLOTS = 7
+SIGNED = 7
 
 WEIGHT_FOR = (
     (WR, NEG_WI, NEG_WJ, NEG_WK),
@@ -35,6 +39,17 @@ WEIGHT_FOR = (
     (WK, NEG_WI, WJ, WR),
 )
 
+ROW_OF_BLOCKS = (NEG_WK, WR, WI, NEG_WI, WR, WJ, WK, NEG_WK, WK, NEG_WJ, NEG_WJ)
+SERVED = 2
+SLOTS = len(ROW_OF_BLOCKS)
+
+
+def slot_of(wanted):
+    for s in range(SLOTS - SERVED + 1):
+        if ROW_OF_BLOCKS[s : s + SERVED] == wanted:
+            return s
+    raise AssertionError("these weights are not neighbours in ROW_OF_BLOCKS")
+
 
 def tile_quaternionlinear_pa_kernel(tc, x, wr, wi, wj, wk, bias, out):
     nc = tc.nc
@@ -42,9 +57,15 @@ def tile_quaternionlinear_pa_kernel(tc, x, wr, wi, wj, wk, bias, out):
     out_rows = out.flatten_outer_dims()
     weights = (wr, wi, wj, wk)
 
-    with tc.tile_pool(name="keep", bufs=1) as keep, tc.tile_pool(name="stage", bufs=3) as stage, tc.tile_pool(
+    with tc.tile_pool(name="keep", bufs=1) as keep, tc.tile_pool(name="stage", bufs=4) as stage, tc.tile_pool(
         name="results", bufs=4
-    ) as results, tc.psum_pool(name="flipped", bufs=4) as flipped, tc.psum_pool(name="sums", bufs=4) as sums:
+    ) as results, tc.psum_pool(name="flipped", bufs=4) as flipped, tc.psum_pool(name="sums", bufs=4) as sums, tc.manual_schedule():
+        bias_row = keep.tile([P, OQ * Q], BF16)
+        nc.vector.memset(bias_row[:], 0.0)
+        nc.scalar.dma_start(out=bias_row[0:1, :], in_=bias.unsqueeze(0))
+        ones = keep.tile([P, P], BF16)
+        nc.vector.memset(ones[:], 1.0)
+
         w_raw = []
         x_raw = []
 
@@ -59,13 +80,10 @@ def tile_quaternionlinear_pa_kernel(tc, x, wr, wi, wj, wk, bias, out):
             nc.sync.dma_start(out=rows[:], in_=x_rows[t * P : (t + 1) * P, :])
             x_raw.append(rows)
 
-        load_weights(0)
         load_x(0)
-        for ob in range(1, O_BLOCKS):
-            load_weights(ob)
         load_x(1)
-        bias_all = keep.tile([P, OQ * Q], BF16)
-        nc.sync.dma_start(out=bias_all[:], in_=bias.partition_broadcast(P))
+        for ob in range(O_BLOCKS):
+            load_weights(ob)
         for t in range(2, ROW_TILES):
             load_x(t)
 
@@ -74,82 +92,107 @@ def tile_quaternionlinear_pa_kernel(tc, x, wr, wi, wj, wk, bias, out):
 
         w_codes = keep.tile([P, O_BLOCKS, SLOTS * P], U32, align_bytes=64)
         w_scales = keep.tile([P, O_BLOCKS, SLOTS * P], U8, align_bytes=64)
+        x_codes = keep.tile([P, ROW_TILES, Q * P], U32, align_bytes=64)
+        x_scales = keep.tile([P, ROW_TILES, Q * P], U8, align_bytes=64)
+        bias_all = keep.tile([P, OQ * Q], BF16)
+        planes = {}
 
-        def transpose_and_group(four):
+        def spread_bias():
+            for b in range(OQ * Q // BANK_BF16):
+                bank = flipped.tile([P, BANK_BF16], BF16, tag="bank")
+                for h in range(BANK_BF16 // MATMUL_COLS):
+                    nc.tensor.matmul(
+                        out=bank[:, h * MATMUL_COLS : (h + 1) * MATMUL_COLS],
+                        lhsT=ones[:],
+                        rhs=bias_row[:, b * BANK_BF16 + h * MATMUL_COLS : b * BANK_BF16 + (h + 1) * MATMUL_COLS],
+                        start=True,
+                        stop=True,
+                    )
+                nc.scalar.copy(out=bias_all[:, b * BANK_BF16 : (b + 1) * BANK_BF16], in_=bank[:])
+
+        def transpose_and_group(four, grouped):
             words = four.bitcast(F32)
-            grouped = stage.tile([P, GROUPED], BF16, align_bytes=64)
-            grouped_words = grouped[:].bitcast(F32).rearrange("p (m r u) -> p m r u", m=Q, u=2)
+            grouped_words = grouped.bitcast(F32).rearrange("p (m r u) -> p m r u", m=Q, u=2)
             for pair in range(2):
-                bank = flipped.tile([P, 2, 2, P], F32)
+                bank = flipped.tile([P, 2, 2, P], F32, tag="bank")
                 for m in range(2):
                     for u in range(2):
                         nc.tensor.transpose(bank[:, m, u, :], words[:, 2 * pair + m, u * P : (u + 1) * P], identity[:])
                 nc.scalar.copy(
                     out=grouped_words[:, 2 * pair : 2 * pair + 2, :, :], in_=bank[:].rearrange("p m u r -> p m r u")
                 )
-            return grouped
 
         def prepare_weights(ob):
-            grouped = transpose_and_group(w_raw[ob][:])
-            nc.vector.quantize_mx(
-                out=w_codes[:, ob, 0 : Q * P].bitcast(FP8X4), scales=w_scales[:, ob, 0 : Q * P], in_=grouped[:]
-            )
-            negated = stage.tile([P, 3 * P * 4], BF16, align_bytes=64)
+            signed = stage.tile([P, SIGNED * MATRIX], BF16, align_bytes=64)
+            transpose_and_group(w_raw[ob][:], signed[:, 0 : Q * MATRIX])
             nc.vector.tensor_scalar(
-                out=negated[:], in0=grouped[:, P * 4 :], scalar1=-1.0, scalar2=None, op0=mybir.AluOpType.mult
+                out=signed[:, NEG_WI * MATRIX :],
+                in0=signed[:, WI * MATRIX : Q * MATRIX],
+                scalar1=-1.0,
+                scalar2=None,
+                op0=mybir.AluOpType.mult,
             )
-            nc.vector.quantize_mx(
-                out=w_codes[:, ob, NEG_WI * P : NEG_WK * P].bitcast(FP8X4),
-                scales=w_scales[:, ob, NEG_WI * P : NEG_WK * P],
-                in_=negated[:, 0 : 2 * P * 4],
-            )
-            nc.vector.quantize_mx(
-                out=w_codes[:, ob, NEG_WK * P : SLOTS * P].bitcast(FP8X4),
-                scales=w_scales[:, ob, NEG_WK * P : SLOTS * P],
-                in_=negated[:, 2 * P * 4 :],
-            )
-
-        def prepare_x(t):
-            planes = stage.tile([P, Q, IQ], BF16)
-            interleaved = x_raw[t][:].rearrange("p (i c) -> p c i", c=Q)
-            nc.vector.tensor_copy(out=planes[:, 0:2, :], in_=interleaved[:, 0:2, :])
-            nc.scalar.copy(out=planes[:, 2:4, :], in_=interleaved[:, 2:4, :])
-            grouped = transpose_and_group(planes[:])
-            x_codes = stage.tile([P, Q * P], U32, align_bytes=64)
-            x_scales = stage.tile([P, Q * P], U8, align_bytes=64)
-            nc.vector.quantize_mx(out=x_codes[:].bitcast(FP8X4), scales=x_scales[:], in_=grouped[:])
-            return x_codes, x_scales
-
-        def multiply(t, x_codes, x_scales):
-            for ob in range(O_BLOCKS):
-                acc = sums.tile([P, Q, P], F32)
-                for c_out in range(Q):
-                    for c_in in range(Q):
-                        slot = WEIGHT_FOR[c_out][c_in]
-                        nc.tensor.matmul_mx(
-                            out=acc[:, c_out, :],
-                            lhsT=x_codes[:, c_in * P : (c_in + 1) * P].bitcast(FP8X4),
-                            lhsT_scale=x_scales[:, c_in * P : (c_in + 1) * P],
-                            rhs=w_codes[:, ob, slot * P : (slot + 1) * P].bitcast(FP8X4),
-                            rhs_scale=w_scales[:, ob, slot * P : (slot + 1) * P],
-                            start=(c_in == 0),
-                            stop=(c_in == Q - 1),
-                        )
-                cols = slice(ob * P * Q, (ob + 1) * P * Q)
-                result = results.tile([P, P * Q], F32)
-                nc.vector.tensor_tensor(
-                    out=result[:].rearrange("p (o c) -> p o c", c=Q),
-                    in0=acc[:].rearrange("p c o -> p o c"),
-                    in1=bias_all[:, cols].rearrange("p (o c) -> p o c", c=Q),
-                    op=mybir.AluOpType.add,
+            for s in range(SLOTS):
+                which = ROW_OF_BLOCKS[s]
+                nc.vector.quantize_mx(
+                    out=w_codes[:, ob, s * P : (s + 1) * P].bitcast(FP8X4),
+                    scales=w_scales[:, ob, s * P : (s + 1) * P],
+                    in_=signed[:, which * MATRIX : (which + 1) * MATRIX],
                 )
-                nc.sync.dma_start(out=out_rows[t * P : (t + 1) * P, cols], in_=result[:])
 
+        def deinterleave(t):
+            separate = stage.tile([P, Q, IQ], BF16)
+            interleaved = x_raw[t][:].rearrange("p (i c) -> p c i", c=Q)
+            nc.vector.tensor_copy(out=separate[:, 0:2, :], in_=interleaved[:, 0:2, :])
+            nc.scalar.copy(out=separate[:, 2:4, :], in_=interleaved[:, 2:4, :])
+            planes[t] = separate
+
+        def quantise_x(t):
+            grouped = stage.tile([P, Q * MATRIX], BF16, align_bytes=64)
+            transpose_and_group(planes[t][:], grouped[:])
+            nc.vector.quantize_mx(out=x_codes[:, t, :].bitcast(FP8X4), scales=x_scales[:, t, :], in_=grouped[:])
+
+        def multiply(t, ob):
+            acc = sums.tile([P, Q * P], F32)
+            for first in range(0, Q, SERVED):
+                for c_in in range(Q):
+                    s = slot_of(tuple(WEIGHT_FOR[c_out][c_in] for c_out in range(first, first + SERVED)))
+                    nc.tensor.matmul_mx(
+                        out=acc[:, first * P : (first + SERVED) * P],
+                        lhsT=x_codes[:, t, c_in * P : (c_in + 1) * P].bitcast(FP8X4),
+                        lhsT_scale=x_scales[:, t, c_in * P : (c_in + 1) * P],
+                        rhs=w_codes[:, ob, s * P : (s + SERVED) * P].bitcast(FP8X4),
+                        rhs_scale=w_scales[:, ob, s * P : (s + SERVED) * P],
+                        start=(c_in == 0),
+                        stop=(c_in == Q - 1),
+                    )
+            cols = slice(ob * P * Q, (ob + 1) * P * Q)
+            result = results.tile([P, P * Q], F32)
+            nc.vector.tensor_tensor(
+                out=result[:].rearrange("p (o c) -> p o c", c=Q),
+                in0=acc[:].rearrange("p (c o) -> p o c", c=Q),
+                in1=bias_all[:, cols].rearrange("p (o c) -> p o c", c=Q),
+                op=mybir.AluOpType.add,
+            )
+            nc.sync.dma_start(out=out_rows[t * P : (t + 1) * P, cols], in_=result[:])
+
+        deinterleave(0)
+        deinterleave(1)
+        quantise_x(0)
         prepare_weights(0)
-        ready = prepare_x(0)
-        for ob in range(1, O_BLOCKS):
-            prepare_weights(ob)
-        for t in range(ROW_TILES):
-            following = prepare_x(t + 1) if t + 1 < ROW_TILES else None
-            multiply(t, ready[0], ready[1])
-            ready = following
+        quantise_x(1)
+        spread_bias()
+
+        for pair in range(PAIRS):
+            here = (2 * pair, 2 * pair + 1)
+            ahead = (2 * pair + 2, 2 * pair + 3) if pair + 1 < PAIRS else ()
+            for ob in range(O_BLOCKS):
+                if pair == 0 and ob + 1 < O_BLOCKS:
+                    prepare_weights(ob + 1)
+                for t in ahead:
+                    if ob == DEINTERLEAVE_AT:
+                        deinterleave(t)
+                    if ob == TRANSPOSE_AT:
+                        quantise_x(t)
+                for t in here:
+                    multiply(t, ob)

@@ -20,6 +20,7 @@ BANK_BF16 = 1024
 MATMUL_COLS = 512
 DEINTERLEAVE_AT = 0
 TRANSPOSE_AT = 2
+SHARED = 2
 
 FLOPS = 2 * ROWS * IQ * OQ * 10
 
@@ -66,23 +67,24 @@ def tile_quaternionlinear_pa_kernel(tc, x, wr, wi, wj, wk, bias, out):
         ones = keep.tile([P, P], BF16)
         nc.vector.memset(ones[:], 1.0)
 
-        w_raw = []
-        x_raw = []
+        w_raw = {}
+        x_raw = {}
 
         def load_weights(ob):
             block = keep.tile([P, Q, IQ], BF16, name="w_raw%d" % ob)
             for m in range(Q):
                 nc.sync.dma_start(out=block[:, m, :], in_=weights[m][ob * P : (ob + 1) * P, :])
-            w_raw.append(block)
+            w_raw[ob] = block
 
         def load_x(t):
             rows = keep.tile([P, IQ * Q], BF16, name="x_raw%d" % t)
             nc.sync.dma_start(out=rows[:], in_=x_rows[t * P : (t + 1) * P, :])
-            x_raw.append(rows)
+            x_raw[t] = rows
 
+        load_weights(0)
         load_x(0)
         load_x(1)
-        for ob in range(O_BLOCKS):
+        for ob in range(1, O_BLOCKS):
             load_weights(ob)
         for t in range(2, ROW_TILES):
             load_x(t)
@@ -96,6 +98,8 @@ def tile_quaternionlinear_pa_kernel(tc, x, wr, wi, wj, wk, bias, out):
         x_scales = keep.tile([P, ROW_TILES, Q * P], U8, align_bytes=64)
         bias_all = keep.tile([P, OQ * Q], BF16)
         planes = {}
+        x_grouped = {}
+        w_signed = {}
 
         def spread_bias():
             for b in range(OQ * Q // BANK_BF16):
@@ -122,9 +126,13 @@ def tile_quaternionlinear_pa_kernel(tc, x, wr, wi, wj, wk, bias, out):
                     out=grouped_words[:, 2 * pair : 2 * pair + 2, :, :], in_=bank[:].rearrange("p m u r -> p m r u")
                 )
 
-        def prepare_weights(ob):
+        def transpose_weights(ob):
             signed = stage.tile([P, SIGNED * MATRIX], BF16, align_bytes=64)
             transpose_and_group(w_raw[ob][:], signed[:, 0 : Q * MATRIX])
+            w_signed[ob] = signed
+
+        def quantise_weights(ob):
+            signed = w_signed[ob]
             nc.vector.tensor_scalar(
                 out=signed[:, NEG_WI * MATRIX :],
                 in0=signed[:, WI * MATRIX : Q * MATRIX],
@@ -132,25 +140,31 @@ def tile_quaternionlinear_pa_kernel(tc, x, wr, wi, wj, wk, bias, out):
                 scalar2=None,
                 op0=mybir.AluOpType.mult,
             )
-            for s in range(SLOTS):
-                which = ROW_OF_BLOCKS[s]
-                nc.vector.quantize_mx(
-                    out=w_codes[:, ob, s * P : (s + 1) * P].bitcast(FP8X4),
-                    scales=w_scales[:, ob, s * P : (s + 1) * P],
-                    in_=signed[:, which * MATRIX : (which + 1) * MATRIX],
-                )
+            for negated in (False, True):
+                for s in range(SLOTS):
+                    which = ROW_OF_BLOCKS[s]
+                    if (which >= NEG_WI) == negated:
+                        nc.vector.quantize_mx(
+                            out=w_codes[:, ob, s * P : (s + 1) * P].bitcast(FP8X4),
+                            scales=w_scales[:, ob, s * P : (s + 1) * P],
+                            in_=signed[:, which * MATRIX : (which + 1) * MATRIX],
+                        )
 
-        def deinterleave(t):
+        def deinterleave(t, on_vector):
             separate = stage.tile([P, Q, IQ], BF16)
             interleaved = x_raw[t][:].rearrange("p (i c) -> p c i", c=Q)
-            nc.vector.tensor_copy(out=separate[:, 0:2, :], in_=interleaved[:, 0:2, :])
-            nc.scalar.copy(out=separate[:, 2:4, :], in_=interleaved[:, 2:4, :])
+            nc.vector.tensor_copy(out=separate[:, 0:on_vector, :], in_=interleaved[:, 0:on_vector, :])
+            if on_vector < Q:
+                nc.scalar.copy(out=separate[:, on_vector:Q, :], in_=interleaved[:, on_vector:Q, :])
             planes[t] = separate
 
-        def quantise_x(t):
+        def transpose_x(t):
             grouped = stage.tile([P, Q * MATRIX], BF16, align_bytes=64)
             transpose_and_group(planes[t][:], grouped[:])
-            nc.vector.quantize_mx(out=x_codes[:, t, :].bitcast(FP8X4), scales=x_scales[:, t, :], in_=grouped[:])
+            x_grouped[t] = grouped
+
+        def quantise_x(t):
+            nc.vector.quantize_mx(out=x_codes[:, t, :].bitcast(FP8X4), scales=x_scales[:, t, :], in_=x_grouped[t][:])
 
         def multiply(t, ob):
             acc = sums.tile([P, Q * P], F32)
@@ -176,23 +190,28 @@ def tile_quaternionlinear_pa_kernel(tc, x, wr, wi, wj, wk, bias, out):
             )
             nc.sync.dma_start(out=out_rows[t * P : (t + 1) * P, cols], in_=result[:])
 
-        deinterleave(0)
-        deinterleave(1)
-        quantise_x(0)
-        prepare_weights(0)
-        quantise_x(1)
+        transpose_weights(0)
         spread_bias()
+        deinterleave(0, Q)
+        transpose_x(0)
+        deinterleave(1, Q)
+        quantise_weights(0)
+        quantise_x(0)
+        transpose_x(1)
+        quantise_x(1)
 
         for pair in range(PAIRS):
             here = (2 * pair, 2 * pair + 1)
             ahead = (2 * pair + 2, 2 * pair + 3) if pair + 1 < PAIRS else ()
             for ob in range(O_BLOCKS):
                 if pair == 0 and ob + 1 < O_BLOCKS:
-                    prepare_weights(ob + 1)
+                    transpose_weights(ob + 1)
+                    quantise_weights(ob + 1)
                 for t in ahead:
                     if ob == DEINTERLEAVE_AT:
-                        deinterleave(t)
+                        deinterleave(t, SHARED)
                     if ob == TRANSPOSE_AT:
+                        transpose_x(t)
                         quantise_x(t)
                 for t in here:
                     multiply(t, ob)

import concourse.mybir as mybir
from concourse.masks import make_identity

F32 = mybir.dt.float32
BF16 = mybir.dt.bfloat16
U32 = mybir.dt.uint32
U8 = mybir.dt.uint8
FP8X4 = mybir.dt.float8_e4m3fn_x4

P = 128
Q = 4
ROWS = 1024
IQ = 512
OQ = 512
ROW_TILES = ROWS // P
PAIRS = ROW_TILES // 2
O_BLOCKS = OQ // P
MATRIX = P * 4
BANK_BF16 = 1024
MATMUL_COLS = 512
DEINTERLEAVE_AT = 0
TRANSPOSE_AT = 2
SHARED = 2

FLOPS = 2 * ROWS * IQ * OQ * 10

WR = 0
WI = 1
WJ = 2
WK = 3
NEG_WI = 4
NEG_WJ = 5
NEG_WK = 6
SIGNED = 7

WEIGHT_FOR = (
    (WR, NEG_WI, NEG_WJ, NEG_WK),
    (WI, WR, NEG_WJ, WK),
    (WJ, WI, WR, NEG_WK),
    (WK, NEG_WI, WJ, WR),
)

ROW_OF_BLOCKS = (NEG_WK, WR, WI, NEG_WI, WR, WJ, WK, NEG_WK, WK, NEG_WJ, NEG_WJ)
SERVED = 2
SLOTS = len(ROW_OF_BLOCKS)


def slot_of(wanted):
    for s in range(SLOTS - SERVED + 1):
        if ROW_OF_BLOCKS[s : s + SERVED] == wanted:
            return s
    raise AssertionError("these weights are not neighbours in ROW_OF_BLOCKS")


def tile_quaternionlinear_pa_kernel(tc, x, wr, wi, wj, wk, bias, out):
    nc = tc.nc
    x_rows = x.flatten_outer_dims()
    out_rows = out.flatten_outer_dims()
    weights = (wr, wi, wj, wk)

    with tc.tile_pool(name="keep", bufs=1) as keep, tc.tile_pool(name="stage", bufs=4) as stage, tc.tile_pool(
        name="results", bufs=4
    ) as results, tc.psum_pool(name="flipped", bufs=4) as flipped, tc.psum_pool(name="sums", bufs=4) as sums, tc.manual_schedule():
        bias_row = keep.tile([P, OQ * Q], BF16)
        nc.vector.memset(bias_row[:], 0.0)
        nc.scalar.dma_start(out=bias_row[0:1, :], in_=bias.unsqueeze(0))
        ones = keep.tile([P, P], BF16)
        nc.vector.memset(ones[:], 1.0)

        w_raw = {}
        x_raw = {}

        def load_weights(ob):
            block = keep.tile([P, Q, IQ], BF16, name="w_raw%d" % ob)
            for m in range(Q):
                nc.sync.dma_start(out=block[:, m, :], in_=weights[m][ob * P : (ob + 1) * P, :])
            w_raw[ob] = block

        def load_x(t):
            rows = keep.tile([P, IQ * Q], BF16, name="x_raw%d" % t)
            nc.sync.dma_start(out=rows[:], in_=x_rows[t * P : (t + 1) * P, :])
            x_raw[t] = rows

        load_weights(0)
        load_x(0)
        load_x(1)
        for ob in range(1, O_BLOCKS):
            load_weights(ob)
        for t in range(2, ROW_TILES):
            load_x(t)

        identity = keep.tile([P, P], F32)
        make_identity(nc, identity[:])

        w_codes = keep.tile([P, O_BLOCKS, SLOTS * P], U32, align_bytes=64)
        w_scales = keep.tile([P, O_BLOCKS, SLOTS * P], U8, align_bytes=64)
        x_codes = keep.tile([P, ROW_TILES, Q * P], U32, align_bytes=64)
        x_scales = keep.tile([P, ROW_TILES, Q * P], U8, align_bytes=64)
        bias_all = keep.tile([P, OQ * Q], BF16)
        planes = {}
        x_grouped = {}
        w_signed = {}

        def spread_bias():
            for b in range(OQ * Q // BANK_BF16):
                bank = flipped.tile([P, BANK_BF16], BF16, tag="bank")
                for h in range(BANK_BF16 // MATMUL_COLS):
                    nc.tensor.matmul(
                        out=bank[:, h * MATMUL_COLS : (h + 1) * MATMUL_COLS],
                        lhsT=ones[:],
                        rhs=bias_row[:, b * BANK_BF16 + h * MATMUL_COLS : b * BANK_BF16 + (h + 1) * MATMUL_COLS],
                        start=True,
                        stop=True,
                    )
                nc.scalar.copy(out=bias_all[:, b * BANK_BF16 : (b + 1) * BANK_BF16], in_=bank[:])

        def transpose_and_group(four, grouped):
            words = four.bitcast(F32)
            grouped_words = grouped.bitcast(F32).rearrange("p (m r u) -> p m r u", m=Q, u=2)
            for pair in range(2):
                bank = flipped.tile([P, 2, 2, P], F32, tag="bank")
                for m in range(2):
                    for u in range(2):
                        nc.tensor.transpose(bank[:, m, u, :], words[:, 2 * pair + m, u * P : (u + 1) * P], identity[:])
                nc.scalar.copy(
                    out=grouped_words[:, 2 * pair : 2 * pair + 2, :, :], in_=bank[:].rearrange("p m u r -> p m r u")
                )

        def transpose_weights(ob):
            signed = stage.tile([P, SIGNED * MATRIX], BF16, align_bytes=64)
            transpose_and_group(w_raw[ob][:], signed[:, 0 : Q * MATRIX])
            w_signed[ob] = signed

        def quantise_weights(ob):
            signed = w_signed[ob]
            nc.vector.tensor_scalar(
                out=signed[:, NEG_WI * MATRIX :],
                in0=signed[:, WI * MATRIX : Q * MATRIX],
                scalar1=-1.0,
                scalar2=None,
                op0=mybir.AluOpType.mult,
            )
            for negated in (False, True):
                for s in range(SLOTS):
                    which = ROW_OF_BLOCKS[s]
                    if (which >= NEG_WI) == negated:
                        nc.vector.quantize_mx(
                            out=w_codes[:, ob, s * P : (s + 1) * P].bitcast(FP8X4),
                            scales=w_scales[:, ob, s * P : (s + 1) * P],
                            in_=signed[:, which * MATRIX : (which + 1) * MATRIX],
                        )

        def deinterleave(t, on_vector):
            separate = stage.tile([P, Q, IQ], BF16)
            interleaved = x_raw[t][:].rearrange("p (i c) -> p c i", c=Q)
            nc.vector.tensor_copy(out=separate[:, 0:on_vector, :], in_=interleaved[:, 0:on_vector, :])
            if on_vector < Q:
                nc.scalar.copy(out=separate[:, on_vector:Q, :], in_=interleaved[:, on_vector:Q, :])
            planes[t] = separate

        def transpose_x(t):
            grouped = stage.tile([P, Q * MATRIX], BF16, align_bytes=64)
            transpose_and_group(planes[t][:], grouped[:])
            x_grouped[t] = grouped

        def quantise_x(t):
            nc.vector.quantize_mx(out=x_codes[:, t, :].bitcast(FP8X4), scales=x_scales[:, t, :], in_=x_grouped[t][:])

        def multiply(t, ob):
            acc = sums.tile([P, Q * P], F32)
            for first in range(0, Q, SERVED):
                for c_in in range(Q):
                    s = slot_of(tuple(WEIGHT_FOR[c_out][c_in] for c_out in range(first, first + SERVED)))
                    nc.tensor.matmul_mx(
                        out=acc[:, first * P : (first + SERVED) * P],
                        lhsT=x_codes[:, t, c_in * P : (c_in + 1) * P].bitcast(FP8X4),
                        lhsT_scale=x_scales[:, t, c_in * P : (c_in + 1) * P],
                        rhs=w_codes[:, ob, s * P : (s + SERVED) * P].bitcast(FP8X4),
                        rhs_scale=w_scales[:, ob, s * P : (s + SERVED) * P],
                        start=(c_in == 0),
                        stop=(c_in == Q - 1),
                    )
            cols = slice(ob * P * Q, (ob + 1) * P * Q)
            result = results.tile([P, P * Q], F32)
            nc.vector.tensor_tensor(
                out=result[:].rearrange("p (o c) -> p o c", c=Q),
                in0=acc[:].rearrange("p (c o) -> p o c", c=Q),
                in1=bias_all[:, cols].rearrange("p (o c) -> p o c", c=Q),
                op=mybir.AluOpType.add,
            )
            nc.sync.dma_start(out=out_rows[t * P : (t + 1) * P, cols], in_=result[:])

        transpose_weights(0)
        spread_bias()
        deinterleave(0, Q)
        transpose_x(0)
        deinterleave(1, Q)
        quantise_weights(0)
        quantise_x(0)
        transpose_x(1)
        quantise_x(1)

        for pair in range(PAIRS):
            here = (2 * pair, 2 * pair + 1)
            ahead = (2 * pair + 2, 2 * pair + 3) if pair + 1 < PAIRS else ()
            for ob in range(O_BLOCKS):
                if pair == 0 and ob + 1 < O_BLOCKS:
                    transpose_weights(ob + 1)
                    quantise_weights(ob + 1)
                for t in ahead:
                    if ob == DEINTERLEAVE_AT:
                        deinterleave(t, SHARED)
                    if ob == TRANSPOSE_AT:
                        transpose_x(t)
                        quantise_x(t)
                for t in here:
                    multiply(t, ob)
